import numpy as np
import ml_dtypes


def mxq(x, axis, fmt="e4m3"):
    dtype, down = {"e4m3": (ml_dtypes.float8_e4m3fn, 7), "e5m2": (ml_dtypes.float8_e5m2, 14)}[fmt]
    v = np.moveaxis(np.asarray(x, np.float32).astype(ml_dtypes.bfloat16).astype(np.float64), axis, -1)
    blocks = v.reshape(v.shape[:-1] + (-1, 32))
    amax = np.abs(blocks).max(-1, keepdims=True)
    byte = np.maximum(np.where(amax > 0, np.frexp(amax)[1] - 1 + 127, 0) - down, 1)
    scale = np.exp2(byte - 127.0)
    codes = (blocks / scale).astype(np.float32).astype(dtype).astype(np.float64)
    return np.moveaxis((codes * scale).reshape(v.shape), -1, axis)


WIDE = False


def mx_kscale(k):
    if not WIDE:
        return np.ones(k)
    levels = np.array([10, -10, 5, -5, 0])
    a = np.random.permutation(np.resize(levels, k // 512 * 4)).reshape(k // 512, 4)
    idx = np.arange(k)
    return np.exp2(a[idx // 512, idx % 128 // 32])


BF16 = ml_dtypes.bfloat16


def bf(x):
    return np.asarray(x, np.float32).astype(BF16)


def f64(x):
    return np.asarray(x).astype(np.float64)


B, T, N, C, WIN, F = 1, 4, 512, 512, 3, 3
NW = T - WIN + 1
K = WIN * N


def setup_inputs():
    s = mx_kscale(N)
    return {"data_temb": bf(np.random.standard_normal((B, T, N, C)) * s[:, None]),
            "adj_mid": bf(np.random.standard_normal((N, K)) / np.sqrt(K) / np.tile(s, WIN)),
            "spatial_emb": bf(np.random.standard_normal((1, 1, N, C)) * 0.3 * s[:, None])}


def reference(data_temb, adj_mid, spatial_emb):
    x = f64(data_temb) + f64(spatial_emb)
    xq = mxq(x, 2, "e4m3")
    idx = np.arange(NW)[:, None] + np.arange(WIN)[None, :]
    return mxq(f64(adj_mid), 1, "e4m3") @ xq[:, idx].reshape(B, NW, K, C)

@@ -1,0 +1,165 @@
+from contextlib import ExitStack
+
+import concourse.mybir as mybir
+from concourse.masks import make_identity
+
+BF16 = mybir.dt.bfloat16
+F32 = mybir.dt.float32
+U32 = mybir.dt.uint32
+U8 = mybir.dt.uint8
+FP8X4 = mybir.dt.float8_e4m3fn_x4
+
+P = 128
+PACK = 4
+T = 4
+NODES = 512
+C = 512
+WIN = 3
+NW = T - WIN + 1
+ROW_TILES = NODES // P
+PAIRS = ROW_TILES // 2
+WHOLE = slice(0, PACK * C)
+HALVES = (slice(0, PACK * C // 2), slice(PACK * C // 2, PACK * C))
+RUN = 4
+
+FLOPS = 2 * NW * NODES * WIN * NODES * C
+
+
+def tile_stsindividuallayer_pa_kernel(tc, data_temb, adj_mid, spatial_emb, out):
+    nc = tc.nc
+    with ExitStack() as ctx:
+        keep = ctx.enter_context(tc.tile_pool(name="keep", bufs=1))
+        results = ctx.enter_context(tc.tile_pool(name="results", bufs=NW * ROW_TILES))
+        banks = ctx.enter_context(tc.psum_pool(name="banks", bufs=8))
+
+        spatial = keep.tile([P, PACK * C], BF16)
+        signal = [keep.tile([P, PACK * C], BF16, name="signal%d" % t) for t in range(T)]
+        adj_rows = keep.tile([P, ROW_TILES * WIN * NODES], BF16)
+
+        def load_nodes(tile, nodes, cols):
+            nc.sync.dma_start(out=tile[:, cols], in_=nodes.rearrange("(p j) c -> p (j c)", j=PACK)[:, cols])
+
+        for cols in HALVES:
+            load_nodes(spatial, spatial_emb[0, 0], cols)
+            load_nodes(signal[0], data_temb[0, 0], cols)
+        load_nodes(signal[1], data_temb[0, 1], WHOLE)
+        for a in range(ROW_TILES):
+            nc.sync.dma_start(
+                out=adj_rows[:, a * WIN * NODES : (a + 1) * WIN * NODES], in_=adj_mid[a * P : (a + 1) * P, :]
+            )
+        load_nodes(signal[2], data_temb[0, 2], WHOLE)
+        load_nodes(signal[3], data_temb[0, 3], WHOLE)
+
+        identity = keep.tile([P, P], F32)
+        make_identity(nc, identity[:])
+
+        summed = [keep.tile([P, PACK * C], BF16, name="summed%d" % t) for t in range(T)]
+        grouped = [keep.tile([P, C * PACK], BF16, name="grouped%d" % t, align_bytes=64) for t in range(T)]
+        x_codes = [keep.tile([P, C], U32, name="x_codes%d" % t, align_bytes=64) for t in range(T)]
+        x_scales = [keep.tile([P, C], U8, name="x_scales%d" % t, align_bytes=64) for t in range(T)]
+
+        def add(t, cols):
+            nc.vector.tensor_tensor(
+                out=summed[t][:, cols], in0=signal[t][:, cols], in1=spatial[:, cols], op=mybir.AluOpType.add
+            )
+
+        def regroup(t):
+            src = summed[t][:].rearrange("p (j c i) -> p c j i", j=PACK, i=RUN)
+            dst = grouped[t][:].rearrange("p (c i j) -> p c j i", i=RUN, j=PACK)
+            half = C // RUN // 2
+            nc.vector.tensor_copy(out=dst[:, :half], in_=src[:, :half])
+            nc.scalar.copy(out=dst[:, half:], in_=src[:, half:])
+
+        def quantise_x(t):
+            nc.vector.quantize_mx(out=x_codes[t][:].bitcast(FP8X4), scales=x_scales[t][:], in_=grouped[t][:])
+
+        adj_words = adj_rows[:].bitcast(F32).rearrange(
+            "p (a g q u) -> p a g u q", a=ROW_TILES, g=WIN, u=2
+        )
+        adj_grouped = keep.tile([P, PAIRS * WIN * 2 * P * PACK], BF16, align_bytes=64)
+        adj_grouped_words = adj_grouped[:].bitcast(F32).rearrange(
+            "p (h g m u) -> p h g m u", h=PAIRS, g=WIN, u=2
+        )
+        adj_codes = keep.tile([P, PAIRS * WIN * 2 * P], U32, align_bytes=64)
+        adj_scales = keep.tile([P, PAIRS * WIN * 2 * P], U8, align_bytes=64)
+
+        flipped = {}
+
+        def transpose_adj(h):
+            for g in range(WIN):
+                flipped[(h, g)] = banks.tile([P, 2, 2 * P], F32, name="flipped%d_%d" % (h, g), tag="bank")
+            for i in range(2):
+                for g in range(WIN):
+                    for u in range(2):
+                        nc.tensor.transpose(
+                            out=flipped[(h, g)][:, u, i * P : (i + 1) * P],
+                            in_=adj_words[:, 2 * h + i, g, u, :],
+                            identity=identity[:],
+                        )
+
+        def copy_adj(h):
+            for g in range(WIN):
+                nc.scalar.copy(out=adj_grouped_words[:, h, g], in_=flipped[(h, g)][:].rearrange("p u m -> p m u"))
+
+        def quantise_adj(h):
+            for g in range(WIN):
+                first = (h * WIN + g) * 2 * P
+                nc.vector.quantize_mx(
+                    out=adj_codes[:, first : first + 2 * P].bitcast(FP8X4),
+                    scales=adj_scales[:, first : first + 2 * P],
+                    in_=adj_grouped[:, first * PACK : (first + 2 * P) * PACK],
+                )
+
+        acc = {}
+
+        def multiply(t):
+            for w in range(NW):
+                j = t - w
+                if 0 <= j < WIN:
+                    for a in range(ROW_TILES):
+                        if j == 0:
+                            acc[(w, a)] = banks.tile([P, C], F32, name="acc%d_%d" % (w, a), tag="bank")
+                        first = ((a // 2) * WIN + j) * 2 * P + (a % 2) * P
+                        nc.tensor.matmul_mx(
+                            out=acc[(w, a)][:],
+                            lhsT=adj_codes[:, first : first + P].bitcast(FP8X4),
+                            lhsT_scale=adj_scales[:, first : first + P],
+                            rhs=x_codes[t][:].bitcast(FP8X4),
+                            rhs_scale=x_scales[t][:],
+                            start=(j == 0),
+                            stop=(j == WIN - 1),
+                        )
+
+        def store(w, a, engine_copy):
+            res = results.tile([P, C], F32, name="res")
+            engine_copy(out=res[:], in_=acc[(w, a)][:])
+            nc.sync.dma_start(out=out[0, w, a * P : (a + 1) * P, :], in_=res[:])
+
+        with tc.manual_schedule():
+            for cols in HALVES:
+                add(0, cols)
+            regroup(0)
+            add(1, WHOLE)
+            quantise_x(0)
+            regroup(1)
+            for h in range(PAIRS):
+                transpose_adj(h)
+            for h in range(PAIRS):
+                copy_adj(h)
+            quantise_x(1)
+            quantise_adj(0)
+            add(2, WHOLE)
+            quantise_adj(1)
+            multiply(0)
+            multiply(1)
+            regroup(2)
+            add(3, WHOLE)
+            quantise_x(2)
+            multiply(2)
+            regroup(3)
+            for a in range(ROW_TILES):
+                store(0, a, nc.scalar.copy)
+            quantise_x(3)
+            multiply(3)
+            for a in range(ROW_TILES):
+                store(1, a, nc.scalar.copy if a % 2 == 0 else nc.vector.tensor_copy)

@@ -112,11 +112,11 @@ def tile_stsindividuallayer_pa_kernel(tc, data_temb, adj_mid, spatial_emb, out):
 
         acc = {}
 
-        def multiply(t):
+        def multiply(t, row_tiles):
             for w in range(NW):
                 j = t - w
                 if 0 <= j < WIN:
-                    for a in range(ROW_TILES):
+                    for a in row_tiles:
                         if j == 0:
                             acc[(w, a)] = banks.tile([P, C], F32, name="acc%d_%d" % (w, a), tag="bank")
                         first = ((a // 2) * WIN + j) * 2 * P + (a % 2) * P
@@ -148,18 +148,20 @@ def tile_stsindividuallayer_pa_kernel(tc, data_temb, adj_mid, spatial_emb, out):
                 copy_adj(h)
             quantise_x(1)
             quantise_adj(0)
+            multiply(0, (0, 1))
+            multiply(1, (0, 1))
             add(2, WHOLE)
             quantise_adj(1)
-            multiply(0)
-            multiply(1)
+            multiply(0, (2, 3))
+            multiply(1, (2, 3))
             regroup(2)
             add(3, WHOLE)
             quantise_x(2)
-            multiply(2)
+            multiply(2, range(ROW_TILES))
             regroup(3)
             for a in range(ROW_TILES):
                 store(0, a, nc.scalar.copy)
             quantise_x(3)
-            multiply(3)
+            multiply(3, range(ROW_TILES))
             for a in range(ROW_TILES):
                 store(1, a, nc.scalar.copy if a % 2 == 0 else nc.vector.tensor_copy)

@@ -18,19 +18,22 @@ WIN = 3
 NW = T - WIN + 1
 ROW_TILES = NODES // P
 PAIRS = ROW_TILES // 2
-WHOLE = slice(0, PACK * C)
-HALVES = (slice(0, PACK * C // 2), slice(PACK * C // 2, PACK * C))
 RUN = 4
 
 FLOPS = 2 * NW * NODES * WIN * NODES * C
+
+HALF = C // 2
+FIRST = (0, HALF)
+SECOND = (HALF, C)
+ACC_BANK = {(0, 0): 0, (0, 1): 1, (1, 0): 6, (1, 1): 7, (0, 2): 2, (0, 3): 3, (1, 2): 4, (1, 3): 5}
 
 
 def tile_stsindividuallayer_pa_kernel(tc, data_temb, adj_mid, spatial_emb, out):
     nc = tc.nc
     with ExitStack() as ctx:
         keep = ctx.enter_context(tc.tile_pool(name="keep", bufs=1))
-        results = ctx.enter_context(tc.tile_pool(name="results", bufs=NW * ROW_TILES))
-        banks = ctx.enter_context(tc.psum_pool(name="banks", bufs=8))
+        results = ctx.enter_context(tc.tile_pool(name="results", bufs=2 * NW * ROW_TILES))
+        banks = ctx.enter_context(tc.psum_pool(name="banks", bufs=1))
 
         spatial = keep.tile([P, PACK * C], BF16)
         signal = [keep.tile([P, PACK * C], BF16, name="signal%d" % t) for t in range(T)]
@@ -39,16 +42,21 @@ def tile_stsindividuallayer_pa_kernel(tc, data_temb, adj_mid, spatial_emb, out):
         def load_nodes(tile, nodes, cols):
             nc.sync.dma_start(out=tile[:, cols], in_=nodes.rearrange("(p j) c -> p (j c)", j=PACK)[:, cols])
 
-        for cols in HALVES:
-            load_nodes(spatial, spatial_emb[0, 0], cols)
-            load_nodes(signal[0], data_temb[0, 0], cols)
-        load_nodes(signal[1], data_temb[0, 1], WHOLE)
-        for a in range(ROW_TILES):
+        def load_adj(a):
             nc.sync.dma_start(
                 out=adj_rows[:, a * WIN * NODES : (a + 1) * WIN * NODES], in_=adj_mid[a * P : (a + 1) * P, :]
             )
-        load_nodes(signal[2], data_temb[0, 2], WHOLE)
-        load_nodes(signal[3], data_temb[0, 3], WHOLE)
+
+        whole = slice(0, PACK * C)
+        node_halves = (slice(0, PACK * C // 2), slice(PACK * C // 2, PACK * C))
+        for cols in node_halves:
+            load_nodes(spatial, spatial_emb[0, 0], cols)
+            load_nodes(signal[0], data_temb[0, 0], cols)
+        load_nodes(signal[1], data_temb[0, 1], whole)
+        for a in range(ROW_TILES):
+            load_adj(a)
+        load_nodes(signal[2], data_temb[0, 2], whole)
+        load_nodes(signal[3], data_temb[0, 3], whole)
 
         identity = keep.tile([P, P], F32)
         make_identity(nc, identity[:])
@@ -58,28 +66,32 @@ def tile_stsindividuallayer_pa_kernel(tc, data_temb, adj_mid, spatial_emb, out):
         x_codes = [keep.tile([P, C], U32, name="x_codes%d" % t, align_bytes=64) for t in range(T)]
         x_scales = [keep.tile([P, C], U8, name="x_scales%d" % t, align_bytes=64) for t in range(T)]
 
-        def add(t, cols):
+        def add_flat(t, cols):
             nc.vector.tensor_tensor(
                 out=summed[t][:, cols], in0=signal[t][:, cols], in1=spatial[:, cols], op=mybir.AluOpType.add
             )
 
-        def regroup(t):
+        def add(t, cols):
+            def view(tile):
+                return tile[:].rearrange("p (j c) -> p j c", j=PACK)[:, :, cols[0] : cols[1]]
+
+            nc.vector.tensor_tensor(out=view(summed[t]), in0=view(signal[t]), in1=view(spatial), op=mybir.AluOpType.add)
+
+        def regroup(t, engine_copy, cols):
             src = summed[t][:].rearrange("p (j c i) -> p c j i", j=PACK, i=RUN)
             dst = grouped[t][:].rearrange("p (c i j) -> p c j i", i=RUN, j=PACK)
-            half = C // RUN // 2
-            nc.vector.tensor_copy(out=dst[:, :half], in_=src[:, :half])
-            nc.scalar.copy(out=dst[:, half:], in_=src[:, half:])
+            engine_copy(out=dst[:, cols[0] // RUN : cols[1] // RUN], in_=src[:, cols[0] // RUN : cols[1] // RUN])
 
-        def quantise_x(t):
-            nc.vector.quantize_mx(out=x_codes[t][:].bitcast(FP8X4), scales=x_scales[t][:], in_=grouped[t][:])
+        def quantise_x(t, cols):
+            nc.vector.quantize_mx(
+                out=x_codes[t][:, cols[0] : cols[1]].bitcast(FP8X4),
+                scales=x_scales[t][:, cols[0] : cols[1]],
+                in_=grouped[t][:, cols[0] * PACK : cols[1] * PACK],
+            )
 
-        adj_words = adj_rows[:].bitcast(F32).rearrange(
-            "p (a g q u) -> p a g u q", a=ROW_TILES, g=WIN, u=2
-        )
+        adj_words = adj_rows[:].bitcast(F32).rearrange("p (a g q u) -> p a g u q", a=ROW_TILES, g=WIN, u=2)
         adj_grouped = keep.tile([P, PAIRS * WIN * 2 * P * PACK], BF16, align_bytes=64)
-        adj_grouped_words = adj_grouped[:].bitcast(F32).rearrange(
-            "p (h g m u) -> p h g m u", h=PAIRS, g=WIN, u=2
-        )
+        adj_grouped_words = adj_grouped[:].bitcast(F32).rearrange("p (h g m u) -> p h g m u", h=PAIRS, g=WIN, u=2)
         adj_codes = keep.tile([P, PAIRS * WIN * 2 * P], U32, align_bytes=64)
         adj_scales = keep.tile([P, PAIRS * WIN * 2 * P], U8, align_bytes=64)
 
@@ -87,7 +99,7 @@ def tile_stsindividuallayer_pa_kernel(tc, data_temb, adj_mid, spatial_emb, out):
 
         def transpose_adj(h):
             for g in range(WIN):
-                flipped[(h, g)] = banks.tile([P, 2, 2 * P], F32, name="flipped%d_%d" % (h, g), tag="bank")
+                flipped[(h, g)] = banks.tile([P, 2, 2 * P], F32, name="flipped%d_%d" % (h, g), tag="bank%d" % (h * WIN + g))
             for i in range(2):
                 for g in range(WIN):
                     for u in range(2):
@@ -97,71 +109,99 @@ def tile_stsindividuallayer_pa_kernel(tc, data_temb, adj_mid, spatial_emb, out):
                             identity=identity[:],
                         )
 
-        def copy_adj(h):
-            for g in range(WIN):
-                nc.scalar.copy(out=adj_grouped_words[:, h, g], in_=flipped[(h, g)][:].rearrange("p u m -> p m u"))
+        def copy_adj(h, g):
+            nc.scalar.copy(out=adj_grouped_words[:, h, g], in_=flipped[(h, g)][:].rearrange("p u m -> p m u"))
 
-        def quantise_adj(h):
-            for g in range(WIN):
-                first = (h * WIN + g) * 2 * P
-                nc.vector.quantize_mx(
-                    out=adj_codes[:, first : first + 2 * P].bitcast(FP8X4),
-                    scales=adj_scales[:, first : first + 2 * P],
-                    in_=adj_grouped[:, first * PACK : (first + 2 * P) * PACK],
-                )
+        def quantise_adj(h, g):
+            first = (h * WIN + g) * 2 * P
+            nc.vector.quantize_mx(
+                out=adj_codes[:, first : first + 2 * P].bitcast(FP8X4),
+                scales=adj_scales[:, first : first + 2 * P],
+                in_=adj_grouped[:, first * PACK : (first + 2 * P) * PACK],
+            )
 
         acc = {}
 
-        def multiply(t, row_tiles):
-            for w in range(NW):
-                j = t - w
-                if 0 <= j < WIN:
-                    for a in row_tiles:
-                        if j == 0:
-                            acc[(w, a)] = banks.tile([P, C], F32, name="acc%d_%d" % (w, a), tag="bank")
-                        first = ((a // 2) * WIN + j) * 2 * P + (a % 2) * P
-                        nc.tensor.matmul_mx(
-                            out=acc[(w, a)][:],
-                            lhsT=adj_codes[:, first : first + P].bitcast(FP8X4),
-                            lhsT_scale=adj_scales[:, first : first + P],
-                            rhs=x_codes[t][:].bitcast(FP8X4),
-                            rhs_scale=x_scales[t][:],
-                            start=(j == 0),
-                            stop=(j == WIN - 1),
-                        )
+        def multiply(t, w, row_tiles, cols):
+            j = t - w
+            for a in row_tiles:
+                if j == 0:
+                    acc[(w, a, cols)] = banks.tile(
+                        [P, HALF], F32, name="acc%d_%d_%d" % (w, a, cols[0]), tag="bank%d" % ACC_BANK[(w, a)]
+                    )
+                first = ((a // 2) * WIN + j) * 2 * P + (a % 2) * P
+                nc.tensor.matmul_mx(
+                    out=acc[(w, a, cols)][:],
+                    lhsT=adj_codes[:, first : first + P].bitcast(FP8X4),
+                    lhsT_scale=adj_scales[:, first : first + P],
+                    rhs=x_codes[t][:, cols[0] : cols[1]].bitcast(FP8X4),
+                    rhs_scale=x_scales[t][:, cols[0] : cols[1]],
+                    start=(j == 0),
+                    stop=(j == WIN - 1),
+                )
 
-        def store(w, a, engine_copy):
-            res = results.tile([P, C], F32, name="res")
-            engine_copy(out=res[:], in_=acc[(w, a)][:])
-            nc.sync.dma_start(out=out[0, w, a * P : (a + 1) * P, :], in_=res[:])
+        def store(w, a, cols, engine_copy):
+            res = results.tile([P, HALF], F32, name="res")
+            engine_copy(out=res[:], in_=acc[(w, a, cols)][:])
+            nc.sync.dma_start(out=out[0, w, a * P : (a + 1) * P, cols[0] : cols[1]], in_=res[:])
 
+        vcopy = nc.vector.tensor_copy
+        scopy = nc.scalar.copy
+        rows = range(ROW_TILES)
         with tc.manual_schedule():
-            for cols in HALVES:
-                add(0, cols)
-            regroup(0)
-            add(1, WHOLE)
-            quantise_x(0)
-            regroup(1)
+            for cols in node_halves:
+                add_flat(0, cols)
+            regroup(0, scopy, SECOND)
+            add_flat(1, whole)
+            regroup(1, scopy, SECOND)
+            regroup(0, vcopy, FIRST)
+            regroup(1, vcopy, FIRST)
+            quantise_x(0, (0, C))
+            quantise_x(1, (0, C))
             for h in range(PAIRS):
                 transpose_adj(h)
             for h in range(PAIRS):
-                copy_adj(h)
-            quantise_x(1)
-            quantise_adj(0)
-            multiply(0, (0, 1))
-            multiply(1, (0, 1))
-            add(2, WHOLE)
-            quantise_adj(1)
-            multiply(0, (2, 3))
-            multiply(1, (2, 3))
-            regroup(2)
-            add(3, WHOLE)
-            quantise_x(2)
-            multiply(2, range(ROW_TILES))
-            regroup(3)
-            for a in range(ROW_TILES):
-                store(0, a, nc.scalar.copy)
-            quantise_x(3)
-            multiply(3, range(ROW_TILES))
-            for a in range(ROW_TILES):
-                store(1, a, nc.scalar.copy if a % 2 == 0 else nc.vector.tensor_copy)
+                for g in range(WIN):
+                    copy_adj(h, g)
+            for g in range(WIN):
+                quantise_adj(0, g)
+            multiply(0, 0, (0, 1), SECOND)
+            multiply(1, 0, (0, 1), SECOND)
+            multiply(1, 1, (0, 1), SECOND)
+            add(2, SECOND)
+            regroup(2, scopy, SECOND)
+            quantise_adj(1, 0)
+            add(3, SECOND)
+            regroup(3, scopy, SECOND)
+            quantise_adj(1, 1)
+            quantise_adj(1, 2)
+            multiply(0, 0, (2, 3), SECOND)
+            multiply(1, 0, (2, 3), SECOND)
+            multiply(1, 1, (2, 3), SECOND)
+            add(2, FIRST)
+            quantise_x(2, SECOND)
+            multiply(2, 0, rows, SECOND)
+            multiply(2, 1, rows, SECOND)
+            regroup(2, vcopy, FIRST)
+            quantise_x(3, SECOND)
+            multiply(3, 1, rows, SECOND)
+            for a in rows:
+                store(0, a, SECOND, scopy)
+            for a in rows:
+                multiply(0, 0, (a,), FIRST)
+                multiply(1, 0, (a,), FIRST)
+            add(3, FIRST)
+            quantise_x(2, FIRST)
+            multiply(2, 0, rows, FIRST)
+            regroup(3, vcopy, FIRST)
+            for a in (0, 1, 2):
+                store(1, a, SECOND, scopy)
+            store(1, 3, SECOND, vcopy)
+            for a in rows:
+                multiply(1, 1, (a,), FIRST)
+                multiply(2, 1, (a,), FIRST)
+            quantise_x(3, FIRST)
+            multiply(3, 1, rows, FIRST)
+            for w in range(NW):
+                for a in rows:
+                    store(w, a, FIRST, vcopy if a % 2 == 0 else scopy)

@@ -18,6 +18,7 @@ WIN = 3
 NW = T - WIN + 1
 ROW_TILES = NODES // P
 PAIRS = ROW_TILES // 2
+WARM_RUN = 3
 RUN = 4
 
 FLOPS = 2 * NW * NODES * WIN * NODES * C
@@ -145,12 +146,18 @@ def tile_stsindividuallayer_pa_kernel(tc, data_temb, adj_mid, spatial_emb, out):
             engine_copy(out=res[:], in_=acc[(w, a, cols)][:])
             nc.sync.dma_start(out=out[0, w, a * P : (a + 1) * P, cols[0] : cols[1]], in_=res[:])
 
+        def warm_up(moving, stationary):
+            for i in range(WARM_RUN):
+                nc.tensor.matmul(out=warm[:], lhsT=stationary, rhs=moving, start=True, stop=True)
+
+        warm = banks.tile([P, C], F32, name="warm", tag="bank7")
         vcopy = nc.vector.tensor_copy
         scopy = nc.scalar.copy
         rows = range(ROW_TILES)
         with tc.manual_schedule():
             for cols in node_halves:
                 add_flat(0, cols)
+                warm_up(signal[0][:, cols.start : cols.start + C], spatial[:, cols.start : cols.start + P])
             regroup(0, scopy, SECOND)
             add_flat(1, whole)
             regroup(1, scopy, SECOND)

@@ -113,12 +113,13 @@ def tile_stsindividuallayer_pa_kernel(tc, data_temb, adj_mid, spatial_emb, out):
         def copy_adj(h, g):
             nc.scalar.copy(out=adj_grouped_words[:, h, g], in_=flipped[(h, g)][:].rearrange("p u m -> p m u"))
 
-        def quantise_adj(h, g):
+        def quantise_adj(h, g, passes):
             first = (h * WIN + g) * 2 * P
+            last = first + passes * 2 * P
             nc.vector.quantize_mx(
-                out=adj_codes[:, first : first + 2 * P].bitcast(FP8X4),
-                scales=adj_scales[:, first : first + 2 * P],
-                in_=adj_grouped[:, first * PACK : (first + 2 * P) * PACK],
+                out=adj_codes[:, first:last].bitcast(FP8X4),
+                scales=adj_scales[:, first:last],
+                in_=adj_grouped[:, first * PACK : last * PACK],
             )
 
         acc = {}
@@ -170,28 +171,27 @@ def tile_stsindividuallayer_pa_kernel(tc, data_temb, adj_mid, spatial_emb, out):
             for h in range(PAIRS):
                 for g in range(WIN):
                     copy_adj(h, g)
-            for g in range(WIN):
-                quantise_adj(0, g)
+            quantise_adj(0, 0, 2)
+            quantise_adj(0, 2, 1)
             multiply(0, 0, (0, 1), SECOND)
             multiply(1, 0, (0, 1), SECOND)
             multiply(1, 1, (0, 1), SECOND)
             add(2, SECOND)
             regroup(2, scopy, SECOND)
-            quantise_adj(1, 0)
             add(3, SECOND)
             regroup(3, scopy, SECOND)
-            quantise_adj(1, 1)
-            quantise_adj(1, 2)
+            quantise_adj(1, 0, 2)
+            quantise_adj(1, 2, 1)
             multiply(0, 0, (2, 3), SECOND)
             multiply(1, 0, (2, 3), SECOND)
             multiply(1, 1, (2, 3), SECOND)
-            add(2, FIRST)
             quantise_x(2, SECOND)
             multiply(2, 0, rows, SECOND)
             multiply(2, 1, rows, SECOND)
-            regroup(2, vcopy, FIRST)
+            add(2, FIRST)
             quantise_x(3, SECOND)
             multiply(3, 1, rows, SECOND)
+            regroup(2, vcopy, FIRST)
             for a in rows:
                 store(0, a, SECOND, scopy)
             for a in rows:

@@ -204,11 +204,11 @@ def tile_stsindividuallayer_pa_kernel(tc, data_temb, adj_mid, spatial_emb, out):
             for a in (0, 1, 2):
                 store(1, a, SECOND, scopy)
             store(1, 3, SECOND, vcopy)
+            quantise_x(3, FIRST)
             for a in rows:
                 multiply(1, 1, (a,), FIRST)
                 multiply(2, 1, (a,), FIRST)
-            quantise_x(3, FIRST)
-            multiply(3, 1, rows, FIRST)
+                multiply(3, 1, (a,), FIRST)
             for w in range(NW):
                 for a in rows:
                     store(w, a, FIRST, vcopy if a % 2 == 0 else scopy)

@@ -201,9 +201,8 @@ def tile_stsindividuallayer_pa_kernel(tc, data_temb, adj_mid, spatial_emb, out):
             quantise_x(2, FIRST)
             multiply(2, 0, rows, FIRST)
             regroup(3, vcopy, FIRST)
-            for a in (0, 1, 2):
+            for a in rows:
                 store(1, a, SECOND, scopy)
-            store(1, 3, SECOND, vcopy)
             quantise_x(3, FIRST)
             for a in rows:
                 multiply(1, 1, (a,), FIRST)

from contextlib import ExitStack

import concourse.mybir as mybir
from concourse.masks import make_identity

BF16 = mybir.dt.bfloat16
F32 = mybir.dt.float32
U32 = mybir.dt.uint32
U8 = mybir.dt.uint8
FP8X4 = mybir.dt.float8_e4m3fn_x4

P = 128
PACK = 4
T = 4
NODES = 512
C = 512
WIN = 3
NW = T - WIN + 1
ROW_TILES = NODES // P
PAIRS = ROW_TILES // 2
WARM_RUN = 3
RUN = 4

FLOPS = 2 * NW * NODES * WIN * NODES * C

HALF = C // 2
FIRST = (0, HALF)
SECOND = (HALF, C)
ACC_BANK = {(0, 0): 0, (0, 1): 1, (1, 0): 6, (1, 1): 7, (0, 2): 2, (0, 3): 3, (1, 2): 4, (1, 3): 5}


def tile_stsindividuallayer_pa_kernel(tc, data_temb, adj_mid, spatial_emb, out):
    nc = tc.nc
    with ExitStack() as ctx:
        keep = ctx.enter_context(tc.tile_pool(name="keep", bufs=1))
        results = ctx.enter_context(tc.tile_pool(name="results", bufs=2 * NW * ROW_TILES))
        banks = ctx.enter_context(tc.psum_pool(name="banks", bufs=1))

        spatial = keep.tile([P, PACK * C], BF16)
        signal = [keep.tile([P, PACK * C], BF16, name="signal%d" % t) for t in range(T)]
        adj_rows = keep.tile([P, ROW_TILES * WIN * NODES], BF16)

        def load_nodes(tile, nodes, cols):
            nc.sync.dma_start(out=tile[:, cols], in_=nodes.rearrange("(p j) c -> p (j c)", j=PACK)[:, cols])

        def load_adj(a):
            nc.sync.dma_start(
                out=adj_rows[:, a * WIN * NODES : (a + 1) * WIN * NODES], in_=adj_mid[a * P : (a + 1) * P, :]
            )

        whole = slice(0, PACK * C)
        node_halves = (slice(0, PACK * C // 2), slice(PACK * C // 2, PACK * C))
        for cols in node_halves:
            load_nodes(spatial, spatial_emb[0, 0], cols)
            load_nodes(signal[0], data_temb[0, 0], cols)
        load_nodes(signal[1], data_temb[0, 1], whole)
        for a in range(ROW_TILES):
            load_adj(a)
        load_nodes(signal[2], data_temb[0, 2], whole)
        load_nodes(signal[3], data_temb[0, 3], whole)

        identity = keep.tile([P, P], F32)
        make_identity(nc, identity[:])

        summed = [keep.tile([P, PACK * C], BF16, name="summed%d" % t) for t in range(T)]
        grouped = [keep.tile([P, C * PACK], BF16, name="grouped%d" % t, align_bytes=64) for t in range(T)]
        x_codes = [keep.tile([P, C], U32, name="x_codes%d" % t, align_bytes=64) for t in range(T)]
        x_scales = [keep.tile([P, C], U8, name="x_scales%d" % t, align_bytes=64) for t in range(T)]

        def add_flat(t, cols):
            nc.vector.tensor_tensor(
                out=summed[t][:, cols], in0=signal[t][:, cols], in1=spatial[:, cols], op=mybir.AluOpType.add
            )

        def add(t, cols):
            def view(tile):
                return tile[:].rearrange("p (j c) -> p j c", j=PACK)[:, :, cols[0] : cols[1]]

            nc.vector.tensor_tensor(out=view(summed[t]), in0=view(signal[t]), in1=view(spatial), op=mybir.AluOpType.add)

        def regroup(t, engine_copy, cols):
            src = summed[t][:].rearrange("p (j c i) -> p c j i", j=PACK, i=RUN)
            dst = grouped[t][:].rearrange("p (c i j) -> p c j i", i=RUN, j=PACK)
            engine_copy(out=dst[:, cols[0] // RUN : cols[1] // RUN], in_=src[:, cols[0] // RUN : cols[1] // RUN])

        def quantise_x(t, cols):
            nc.vector.quantize_mx(
                out=x_codes[t][:, cols[0] : cols[1]].bitcast(FP8X4),
                scales=x_scales[t][:, cols[0] : cols[1]],
                in_=grouped[t][:, cols[0] * PACK : cols[1] * PACK],
            )

        adj_words = adj_rows[:].bitcast(F32).rearrange("p (a g q u) -> p a g u q", a=ROW_TILES, g=WIN, u=2)
        adj_grouped = keep.tile([P, PAIRS * WIN * 2 * P * PACK], BF16, align_bytes=64)
        adj_grouped_words = adj_grouped[:].bitcast(F32).rearrange("p (h g m u) -> p h g m u", h=PAIRS, g=WIN, u=2)
        adj_codes = keep.tile([P, PAIRS * WIN * 2 * P], U32, align_bytes=64)
        adj_scales = keep.tile([P, PAIRS * WIN * 2 * P], U8, align_bytes=64)

        flipped = {}

        def transpose_adj(h):
            for g in range(WIN):
                flipped[(h, g)] = banks.tile([P, 2, 2 * P], F32, name="flipped%d_%d" % (h, g), tag="bank%d" % (h * WIN + g))
            for i in range(2):
                for g in range(WIN):
                    for u in range(2):
                        nc.tensor.transpose(
                            out=flipped[(h, g)][:, u, i * P : (i + 1) * P],
                            in_=adj_words[:, 2 * h + i, g, u, :],
                            identity=identity[:],
                        )

        def copy_adj(h, g):
            nc.scalar.copy(out=adj_grouped_words[:, h, g], in_=flipped[(h, g)][:].rearrange("p u m -> p m u"))

        def quantise_adj(h, g, passes):
            first = (h * WIN + g) * 2 * P
            last = first + passes * 2 * P
            nc.vector.quantize_mx(
                out=adj_codes[:, first:last].bitcast(FP8X4),
                scales=adj_scales[:, first:last],
                in_=adj_grouped[:, first * PACK : last * PACK],
            )

        acc = {}

        def multiply(t, w, row_tiles, cols):
            j = t - w
            for a in row_tiles:
                if j == 0:
                    acc[(w, a, cols)] = banks.tile(
                        [P, HALF], F32, name="acc%d_%d_%d" % (w, a, cols[0]), tag="bank%d" % ACC_BANK[(w, a)]
                    )
                first = ((a // 2) * WIN + j) * 2 * P + (a % 2) * P
                nc.tensor.matmul_mx(
                    out=acc[(w, a, cols)][:],
                    lhsT=adj_codes[:, first : first + P].bitcast(FP8X4),
                    lhsT_scale=adj_scales[:, first : first + P],
                    rhs=x_codes[t][:, cols[0] : cols[1]].bitcast(FP8X4),
                    rhs_scale=x_scales[t][:, cols[0] : cols[1]],
                    start=(j == 0),
                    stop=(j == WIN - 1),
                )

        def store(w, a, cols, engine_copy):
            res = results.tile([P, HALF], F32, name="res")
            engine_copy(out=res[:], in_=acc[(w, a, cols)][:])
            nc.sync.dma_start(out=out[0, w, a * P : (a + 1) * P, cols[0] : cols[1]], in_=res[:])

        def warm_up(moving, stationary):
            for i in range(WARM_RUN):
                nc.tensor.matmul(out=warm[:], lhsT=stationary, rhs=moving, start=True, stop=True)

        warm = banks.tile([P, C], F32, name="warm", tag="bank7")
        vcopy = nc.vector.tensor_copy
        scopy = nc.scalar.copy
        rows = range(ROW_TILES)
        with tc.manual_schedule():
            for cols in node_halves:
                add_flat(0, cols)
                warm_up(signal[0][:, cols.start : cols.start + C], spatial[:, cols.start : cols.start + P])
            regroup(0, scopy, SECOND)
            add_flat(1, whole)
            regroup(1, scopy, SECOND)
            regroup(0, vcopy, FIRST)
            regroup(1, vcopy, FIRST)
            quantise_x(0, (0, C))
            quantise_x(1, (0, C))
            for h in range(PAIRS):
                transpose_adj(h)
            for h in range(PAIRS):
                for g in range(WIN):
                    copy_adj(h, g)
            quantise_adj(0, 0, 2)
            quantise_adj(0, 2, 1)
            multiply(0, 0, (0, 1), SECOND)
            multiply(1, 0, (0, 1), SECOND)
            multiply(1, 1, (0, 1), SECOND)
            add(2, SECOND)
            regroup(2, scopy, SECOND)
            add(3, SECOND)
            regroup(3, scopy, SECOND)
            quantise_adj(1, 0, 2)
            quantise_adj(1, 2, 1)
            multiply(0, 0, (2, 3), SECOND)
            multiply(1, 0, (2, 3), SECOND)
            multiply(1, 1, (2, 3), SECOND)
            quantise_x(2, SECOND)
            multiply(2, 0, rows, SECOND)
            multiply(2, 1, rows, SECOND)
            add(2, FIRST)
            quantise_x(3, SECOND)
            multiply(3, 1, rows, SECOND)
            regroup(2, vcopy, FIRST)
            for a in rows:
                store(0, a, SECOND, scopy)
            for a in rows:
                multiply(0, 0, (a,), FIRST)
                multiply(1, 0, (a,), FIRST)
            add(3, FIRST)
            quantise_x(2, FIRST)
            multiply(2, 0, rows, FIRST)
            regroup(3, vcopy, FIRST)
            for a in rows:
                store(1, a, SECOND, scopy)
            quantise_x(3, FIRST)
            for a in rows:
                multiply(1, 1, (a,), FIRST)
                multiply(2, 1, (a,), FIRST)
                multiply(3, 1, (a,), FIRST)
            for w in range(NW):
                for a in rows:
                    store(w, a, FIRST, vcopy if a % 2 == 0 else scopy)
